import numpy as np
import ml_dtypes


def mxq(x, axis, fmt="e4m3"):
    dtype, down = {"e4m3": (ml_dtypes.float8_e4m3fn, 7), "e5m2": (ml_dtypes.float8_e5m2, 14)}[fmt]
    v = np.moveaxis(np.asarray(x, np.float32).astype(ml_dtypes.bfloat16).astype(np.float64), axis, -1)
    blocks = v.reshape(v.shape[:-1] + (-1, 32))
    amax = np.abs(blocks).max(-1, keepdims=True)
    byte = np.maximum(np.where(amax > 0, np.frexp(amax)[1] - 1 + 127, 0) - down, 1)
    scale = np.exp2(byte - 127.0)
    codes = (blocks / scale).astype(np.float32).astype(dtype).astype(np.float64)
    return np.moveaxis((codes * scale).reshape(v.shape), -1, axis)


WIDE = False


def mx_kscale(k):
    if not WIDE:
        return np.ones(k)
    levels = np.array([10, -10, 5, -5, 0])
    a = np.random.permutation(np.resize(levels, k // 512 * 4)).reshape(k // 512, 4)
    idx = np.arange(k)
    return np.exp2(a[idx // 512, idx % 128 // 32])


BF16 = ml_dtypes.bfloat16


def bf(x):
    return np.asarray(x, np.float32).astype(BF16)


def f64(x):
    return np.asarray(x).astype(np.float64)


B, D, P, C, DEPTH = 4096, 1024, 512, 128, 2
INT = (1 << DEPTH) - 1
TOT = INT + INT + 1
SIGMA = 1.0


def path_probs(th):
    prob = np.ones((1, th.shape[1]))
    probs = [prob]
    off = 0
    for d in range(DEPTH):
        n = 1 << d
        t = th[off:off + n]
        left = prob * (1.0 + t) * 0.5
        right = prob * (1.0 - t) * 0.5
        prob = np.stack([left, right], axis=1).reshape(n + n, -1)
        probs.append(prob)
        off += n
    return np.concatenate(probs, axis=0)


def setup_inputs():
    s, t = mx_kscale(D), mx_kscale(P)
    return {"X": bf(np.random.standard_normal((B, D)) * s),
            "Z": bf(np.random.standard_normal((P, D)) * 0.25 * P / np.sqrt(D) * t[:, None] / s),
            "W": bf(np.random.standard_normal((C * TOT, P)) * 4.0 / np.sqrt(P) / t),
            "V": bf(np.random.standard_normal((C * TOT, P)) * 4.0 / np.sqrt(P) / t),
            "th": bf(np.tanh(1.5 * np.random.standard_normal((INT, B))))}


def reference(X, Z, W, V, th):
    Xp = (mxq(f64(Z), 1, "e4m3") @ mxq(f64(X), 1, "e4m3").T) / P
    Xq = mxq(Xp, 0, "e4m3")
    WX = (mxq(f64(W), 1, "e4m3") @ Xq).reshape(TOT, C, B)
    VX = (mxq(f64(V), 1, "e4m3") @ Xq).reshape(TOT, C, B)
    probs = path_probs(f64(th))
    return np.sum(probs[:, None, :] * WX * np.tanh(SIGMA * VX), axis=0)

@@ -1,0 +1,257 @@
+from contextlib import ExitStack
+
+import concourse.mybir as mybir
+from concourse.masks import make_identity
+
+F32 = mybir.dt.float32
+BF16 = mybir.dt.bfloat16
+U32 = mybir.dt.uint32
+U8 = mybir.dt.uint8
+FP8X4 = mybir.dt.float8_e4m3fn_x4
+ACT = mybir.ActivationFunctionType
+ALU = mybir.AluOpType
+
+P = 128
+PACK = 4
+K_PASS = P * PACK
+BANK = 512
+
+SAMPLES, FEATURES, PROJECTED, CLASSES = 4096, 1024, 512, 128
+INTERNAL, NODES = 3, 7
+SAMPLE_TILES = SAMPLES // P
+TILES_PER_LOAD = 4
+X_PASSES = FEATURES // K_PASS
+LOW_NODES = BANK // CLASSES
+
+LOW_WIDTHS = (512,)
+HIGH_WIDTHS = (256, 128)
+
+X_LEAD = 4
+XP_LEAD = 2
+SUM_LAG = 1
+OUT_LAG = 3
+
+FLOPS = 2 * PROJECTED * FEATURES * SAMPLES + 2 * 2 * NODES * CLASSES * PROJECTED * SAMPLES
+
+
+def tile_bonsailayer_pa_t_kernel(tc, X, Z, W, V, th, out):
+    nc = tc.nc
+    with ExitStack() as ctx:
+        keep = ctx.enter_context(tc.tile_pool(name="keep", bufs=1))
+        stage = ctx.enter_context(tc.tile_pool(name="stage", bufs=3))
+        codes_pool = ctx.enter_context(tc.tile_pool(name="codes", bufs=X_LEAD + 2))
+        work = ctx.enter_context(tc.tile_pool(name="work", bufs=3))
+        score_pool = ctx.enter_context(tc.tile_pool(name="score", bufs=OUT_LAG + 2))
+        words_psum = ctx.enter_context(tc.psum_pool(name="words_psum", bufs=2))
+        xp_psum = ctx.enter_context(tc.psum_pool(name="xp_psum", bufs=1))
+        vx_psum = ctx.enter_context(tc.psum_pool(name="vx_psum", bufs=2))
+        wx_psum = ctx.enter_context(tc.psum_pool(name="wx_psum", bufs=2))
+        out_psum = ctx.enter_context(tc.psum_pool(name="out_psum", bufs=1))
+        ctx.enter_context(tc.manual_schedule())
+
+        th_rows = keep.tile([P, P], BF16)
+        nc.vector.memset(th_rows[:], 0.0)
+        nc.sync.dma_start(
+            out=th_rows[0 : INTERNAL * SAMPLE_TILES, :],
+            in_=th.rearrange("n (i p) -> (n i) p", p=P),
+        )
+        z_rows = keep.tile([P, PACK, FEATURES], BF16)
+        nc.sync.dma_start(
+            out=z_rows[:].rearrange("p (u e) d -> p u e d", e=2),
+            in_=Z.rearrange("(u p e) d -> p u e d", u=2, e=2),
+        )
+        x_loads = X.rearrange("(g j p) d -> g p j d", j=TILES_PER_LOAD, p=P)
+        x_rows = []
+        for g in range(SAMPLE_TILES // TILES_PER_LOAD):
+            x_rows.append(keep.tile([P, TILES_PER_LOAD, FEATURES], BF16, name="x_rows%d" % g))
+        nc.sync.dma_start(out=x_rows[0][:], in_=x_loads[0])
+        vw_rows = keep.tile([P, 2 * NODES, PROJECTED], BF16)
+        nc.sync.dma_start(out=vw_rows[:, 0:NODES, :], in_=V.rearrange("(n p) k -> p n k", p=P))
+        nc.sync.dma_start(out=vw_rows[:, NODES:, :], in_=W.rearrange("(n p) k -> p n k", p=P))
+        for g in range(1, SAMPLE_TILES // TILES_PER_LOAD):
+            nc.sync.dma_start(out=x_rows[g][:], in_=x_loads[g])
+
+        identity = keep.tile([P, P], F32)
+        make_identity(nc, identity[:])
+
+        th_f32 = keep.tile([P, P], F32)
+        nc.vector.tensor_copy(out=th_f32[:], in_=th_rows[:])
+        th_bank = words_psum.tile([P, P], F32, tag="words")
+        nc.tensor.transpose(th_bank[:], th_f32[:], identity[:])
+        go_left = keep.tile([P, INTERNAL, SAMPLE_TILES], F32)
+        go_right = keep.tile([P, INTERNAL, SAMPLE_TILES], F32)
+        nc.vector.tensor_scalar(
+            out=go_left[:].rearrange("p n i -> p (n i)"), in0=th_bank[:, 0 : INTERNAL * SAMPLE_TILES],
+            scalar1=0.5, scalar2=0.5, op0=ALU.mult, op1=ALU.add,
+        )
+        nc.vector.tensor_scalar(
+            out=go_right[:].rearrange("p n i -> p (n i)"), in0=th_bank[:, 0 : INTERNAL * SAMPLE_TILES],
+            scalar1=-0.5, scalar2=0.5, op0=ALU.mult, op1=ALU.add,
+        )
+        prob = keep.tile([P, NODES, SAMPLE_TILES], F32)
+        nc.vector.memset(prob[:, 0, :], 1.0)
+        for n in range(INTERNAL):
+            nc.vector.tensor_tensor(
+                out=prob[:, 2 * n + 1, :], in0=prob[:, n, :], in1=go_left[:, n, :], op=ALU.mult
+            )
+            nc.vector.tensor_tensor(
+                out=prob[:, 2 * n + 2, :], in0=prob[:, n, :], in1=go_right[:, n, :], op=ALU.mult
+            )
+
+        def quantise_four_blocks(blocks, codes, scales):
+            bank = words_psum.tile([P, 2, 2, P], F32, tag="words")
+            for slot in range(2):
+                for u in range(2):
+                    nc.tensor.transpose(bank[:, slot, u, :], blocks[2 * slot + u], identity[:])
+            grouped = stage.tile([P, 2 * P * PACK], BF16, tag="grouped", align_bytes=64)
+            nc.scalar.copy(
+                out=grouped[:].bitcast(F32).rearrange("p (s r u) -> p s r u", s=2, u=2),
+                in_=bank[:].rearrange("p s u r -> p s r u"),
+            )
+            nc.vector.quantize_mx(out=codes.bitcast(FP8X4), scales=scales, in_=grouped[:])
+
+        z_codes = keep.tile([P, PACK * X_PASSES * P], U32, align_bytes=64)
+        z_scales = keep.tile([P, PACK * X_PASSES * P], U8, align_bytes=64)
+        for t in range(PACK):
+            z_words = z_rows[:, t, :].bitcast(F32)
+            cols = slice(t * X_PASSES * P, (t + 1) * X_PASSES * P)
+            quantise_four_blocks(
+                [z_words[:, w * P : (w + 1) * P] for w in range(4)], z_codes[:, cols], z_scales[:, cols]
+            )
+
+        x_mx, xp_mx, products, scores, out_banks = {}, {}, {}, {}, {}
+
+        def quantise_x(i):
+            x_words = x_rows[i // TILES_PER_LOAD][:, i % TILES_PER_LOAD, :].bitcast(F32)
+            x_codes = codes_pool.tile([P, X_PASSES * P], U32, tag="x_codes", align_bytes=64)
+            x_scales = codes_pool.tile([P, X_PASSES * P], U8, tag="x_scales", align_bytes=64)
+            quantise_four_blocks(
+                [x_words[:, w * P : (w + 1) * P] for w in range(4)], x_codes[:], x_scales[:]
+            )
+            x_mx[i] = (x_codes, x_scales)
+
+        def project(i):
+            x_codes, x_scales = x_mx[i]
+            bank = xp_psum.tile([P, PACK, P], F32, tag="xp")
+            for t in range(PACK):
+                for c in range(X_PASSES):
+                    z_cols = slice((t * X_PASSES + c) * P, (t * X_PASSES + c + 1) * P)
+                    x_cols = slice(c * P, (c + 1) * P)
+                    nc.tensor.matmul_mx(
+                        out=bank[:, t, :],
+                        lhsT=z_codes[:, z_cols].bitcast(FP8X4),
+                        lhsT_scale=z_scales[:, z_cols],
+                        rhs=x_codes[:, x_cols].bitcast(FP8X4),
+                        rhs_scale=x_scales[:, x_cols],
+                        start=(c == 0),
+                        stop=(c == X_PASSES - 1),
+                    )
+            grouped = stage.tile([P, P, PACK], BF16, tag="xp_grouped", align_bytes=64)
+            nc.scalar.activation(
+                out=grouped[:], in_=bank[:].rearrange("p t b -> p b t"), func=ACT.Copy, scale=1.0 / PROJECTED
+            )
+            xp_codes = codes_pool.tile([P, P], U32, tag="xp_codes", align_bytes=64)
+            xp_scales = codes_pool.tile([P, P], U8, tag="xp_scales", align_bytes=64)
+            nc.vector.quantize_mx(
+                out=xp_codes[:].bitcast(FP8X4), scales=xp_scales[:], in_=grouped[:].rearrange("p b t -> p (b t)")
+            )
+            xp_mx[i] = (xp_codes, xp_scales)
+
+        def multiply_nodes(bank, i, first_row_tile, widths):
+            xp_codes, xp_scales = xp_mx[i]
+            done = 0
+            for width in widths:
+                vw_cols = slice(first_row_tile * P + done, first_row_tile * P + done + width)
+                nc.tensor.matmul_mx(
+                    out=bank[:, done : done + width],
+                    lhsT=xp_codes[:].bitcast(FP8X4),
+                    lhsT_scale=xp_scales[:],
+                    rhs=vw_codes[:, vw_cols].bitcast(FP8X4),
+                    rhs_scale=vw_scales[:, vw_cols],
+                    start=True,
+                    stop=True,
+                )
+                done += width
+
+        def score_nodes(i):
+            vx_low = vx_psum.tile([P, BANK], F32, tag="vx")
+            vx_high = vx_psum.tile([P, BANK], F32, tag="vx")
+            wx_low = wx_psum.tile([P, BANK], F32, tag="wx")
+            wx_high = wx_psum.tile([P, BANK], F32, tag="wx")
+            multiply_nodes(vx_low, i, 0, LOW_WIDTHS)
+            multiply_nodes(vx_high, i, LOW_NODES, HIGH_WIDTHS)
+            multiply_nodes(wx_low, i, NODES, LOW_WIDTHS)
+            multiply_nodes(wx_high, i, NODES + LOW_NODES, HIGH_WIDTHS)
+            tanh_vx = work.tile([P, NODES * CLASSES], F32, tag="tanh_vx")
+            nc.scalar.activation(out=tanh_vx[:, 0:BANK], in_=vx_low[:], func=ACT.Tanh)
+            nc.scalar.activation(
+                out=tanh_vx[:, BANK:], in_=vx_high[:, 0 : NODES * CLASSES - BANK], func=ACT.Tanh
+            )
+            product = work.tile([P, NODES * CLASSES], F32, tag="product")
+            for n in range(NODES):
+                wx = wx_low if n < LOW_NODES else wx_high
+                bank_cols = slice((n % LOW_NODES) * CLASSES, (n % LOW_NODES + 1) * CLASSES)
+                node_cols = slice(n * CLASSES, (n + 1) * CLASSES)
+                nc.vector.scalar_tensor_tensor(
+                    out=product[:, node_cols],
+                    in0=wx[:, bank_cols],
+                    scalar=prob[:, n, i : i + 1],
+                    in1=tanh_vx[:, node_cols],
+                    op0=ALU.mult,
+                    op1=ALU.mult,
+                )
+            products[i] = product
+
+        def sum_nodes(i):
+            score = score_pool.tile([P, CLASSES], F32, tag="score")
+            nc.vector.tensor_reduce(
+                out=score[:],
+                in_=products[i][:].rearrange("p (n c) -> p c n", n=NODES),
+                axis=mybir.AxisListType.X,
+                op=ALU.add,
+            )
+            scores[i] = score
+
+        def transpose_score(i):
+            g, j = divmod(i, TILES_PER_LOAD)
+            if j == 0:
+                out_bank = out_psum.tile([P, TILES_PER_LOAD, P], F32, tag="out")
+                out_banks[g] = out_bank
+            nc.tensor.transpose(out_banks[g][:, j, :], scores[i][:], identity[:])
+            if j == TILES_PER_LOAD - 1:
+                out_sb = work.tile([P, TILES_PER_LOAD * P], F32, tag="out_sb")
+                nc.scalar.copy(out=out_sb[:], in_=out_banks[g][:].rearrange("p j b -> p (j b)"))
+                nc.sync.dma_start(
+                    out=out[:, g * TILES_PER_LOAD * P : (g + 1) * TILES_PER_LOAD * P], in_=out_sb[:]
+                )
+
+        def is_tile(i):
+            return 0 <= i < SAMPLE_TILES
+
+        def pipeline_step(step):
+            if is_tile(step + X_LEAD):
+                quantise_x(step + X_LEAD)
+            if is_tile(step - OUT_LAG):
+                transpose_score(step - OUT_LAG)
+            if is_tile(step + XP_LEAD):
+                project(step + XP_LEAD)
+            if is_tile(step):
+                score_nodes(step)
+            if is_tile(step - SUM_LAG):
+                sum_nodes(step - SUM_LAG)
+
+        for step in range(-X_LEAD, 0):
+            pipeline_step(step)
+
+        vw_codes = keep.tile([P, 2 * NODES * P], U32, align_bytes=64)
+        vw_scales = keep.tile([P, 2 * NODES * P], U8, align_bytes=64)
+        for pair in range(NODES):
+            blocks = []
+            for r in (2 * pair, 2 * pair + 1):
+                vw_words = vw_rows[:, r, :].bitcast(F32)
+                blocks.extend([vw_words[:, 0:P], vw_words[:, P : 2 * P]])
+            cols = slice(2 * pair * P, (2 * pair + 2) * P)
+            quantise_four_blocks(blocks, vw_codes[:, cols], vw_scales[:, cols])
+
+        for step in range(0, SAMPLE_TILES + OUT_LAG):
+            pipeline_step(step)

@@ -26,10 +26,12 @@ LOW_NODES = BANK // CLASSES
 LOW_WIDTHS = (512,)
 HIGH_WIDTHS = (256, 128)
 
+FOLDS = ((0, 3), (3, 2), (5, 1))
+
 X_LEAD = 4
 XP_LEAD = 2
-SUM_LAG = 1
-OUT_LAG = 3
+FOLD_LAG = 1
+OUT_LAG = 5
 
 FLOPS = 2 * PROJECTED * FEATURES * SAMPLES + 2 * 2 * NODES * CLASSES * PROJECTED * SAMPLES
 
@@ -41,7 +43,7 @@ def tile_bonsailayer_pa_t_kernel(tc, X, Z, W, V, th, out):
         stage = ctx.enter_context(tc.tile_pool(name="stage", bufs=3))
         codes_pool = ctx.enter_context(tc.tile_pool(name="codes", bufs=X_LEAD + 2))
         work = ctx.enter_context(tc.tile_pool(name="work", bufs=3))
-        score_pool = ctx.enter_context(tc.tile_pool(name="score", bufs=OUT_LAG + 2))
+        product_pool = ctx.enter_context(tc.tile_pool(name="product", bufs=OUT_LAG + 2))
         words_psum = ctx.enter_context(tc.psum_pool(name="words_psum", bufs=2))
         xp_psum = ctx.enter_context(tc.psum_pool(name="xp_psum", bufs=1))
         vx_psum = ctx.enter_context(tc.psum_pool(name="vx_psum", bufs=2))
@@ -119,7 +121,7 @@ def tile_bonsailayer_pa_t_kernel(tc, X, Z, W, V, th, out):
                 [z_words[:, w * P : (w + 1) * P] for w in range(4)], z_codes[:, cols], z_scales[:, cols]
             )
 
-        x_mx, xp_mx, products, scores, out_banks = {}, {}, {}, {}, {}
+        x_mx, xp_mx, products, out_banks = {}, {}, {}, {}
 
         def quantise_x(i):
             x_words = x_rows[i // TILES_PER_LOAD][:, i % TILES_PER_LOAD, :].bitcast(F32)
@@ -187,7 +189,7 @@ def tile_bonsailayer_pa_t_kernel(tc, X, Z, W, V, th, out):
             nc.scalar.activation(
                 out=tanh_vx[:, BANK:], in_=vx_high[:, 0 : NODES * CLASSES - BANK], func=ACT.Tanh
             )
-            product = work.tile([P, NODES * CLASSES], F32, tag="product")
+            product = product_pool.tile([P, NODES * CLASSES], F32, tag="product")
             for n in range(NODES):
                 wx = wx_low if n < LOW_NODES else wx_high
                 bank_cols = slice((n % LOW_NODES) * CLASSES, (n % LOW_NODES + 1) * CLASSES)
@@ -202,22 +204,19 @@ def tile_bonsailayer_pa_t_kernel(tc, X, Z, W, V, th, out):
                 )
             products[i] = product
 
-        def sum_nodes(i):
-            score = score_pool.tile([P, CLASSES], F32, tag="score")
-            nc.vector.tensor_reduce(
-                out=score[:],
-                in_=products[i][:].rearrange("p (n c) -> p c n", n=NODES),
-                axis=mybir.AxisListType.X,
-                op=ALU.add,
+        def fold_nodes(i, first, count):
+            low = slice(first * CLASSES, (first + count) * CLASSES)
+            high = slice((first + count) * CLASSES, (first + 2 * count) * CLASSES)
+            nc.vector.tensor_tensor(
+                out=products[i][:, high], in0=products[i][:, low], in1=products[i][:, high], op=ALU.add
             )
-            scores[i] = score
 
         def transpose_score(i):
             g, j = divmod(i, TILES_PER_LOAD)
             if j == 0:
                 out_bank = out_psum.tile([P, TILES_PER_LOAD, P], F32, tag="out")
                 out_banks[g] = out_bank
-            nc.tensor.transpose(out_banks[g][:, j, :], scores[i][:], identity[:])
+            nc.tensor.transpose(out_banks[g][:, j, :], products[i][:, (NODES - 1) * CLASSES :], identity[:])
             if j == TILES_PER_LOAD - 1:
                 out_sb = work.tile([P, TILES_PER_LOAD * P], F32, tag="out_sb")
                 nc.scalar.copy(out=out_sb[:], in_=out_banks[g][:].rearrange("p j b -> p (j b)"))
@@ -237,8 +236,9 @@ def tile_bonsailayer_pa_t_kernel(tc, X, Z, W, V, th, out):
                 project(step + XP_LEAD)
             if is_tile(step):
                 score_nodes(step)
-            if is_tile(step - SUM_LAG):
-                sum_nodes(step - SUM_LAG)
+            for f, (first, count) in enumerate(FOLDS):
+                if is_tile(step - FOLD_LAG - f):
+                    fold_nodes(step - FOLD_LAG - f, first, count)
 
         for step in range(-X_LEAD, 0):
             pipeline_step(step)

@@ -204,10 +204,10 @@ def tile_bonsailayer_pa_t_kernel(tc, X, Z, W, V, th, out):
                 )
             products[i] = product
 
-        def fold_nodes(i, first, count):
+        def fold_nodes(engine, i, first, count):
             low = slice(first * CLASSES, (first + count) * CLASSES)
             high = slice((first + count) * CLASSES, (first + 2 * count) * CLASSES)
-            nc.vector.tensor_tensor(
+            engine.tensor_tensor(
                 out=products[i][:, high], in0=products[i][:, low], in1=products[i][:, high], op=ALU.add
             )
 
@@ -238,7 +238,7 @@ def tile_bonsailayer_pa_t_kernel(tc, X, Z, W, V, th, out):
                 score_nodes(step)
             for f, (first, count) in enumerate(FOLDS):
                 if is_tile(step - FOLD_LAG - f):
-                    fold_nodes(step - FOLD_LAG - f, first, count)
+                    fold_nodes(nc.gpsimd if f == 0 else nc.vector, step - FOLD_LAG - f, first, count)
 
         for step in range(-X_LEAD, 0):
             pipeline_step(step)

@@ -29,9 +29,12 @@ HIGH_WIDTHS = (256, 128)
 FOLDS = ((0, 3), (3, 2), (5, 1))
 
 X_LEAD = 4
+XQ_LEAD = 3
 XP_LEAD = 2
 FOLD_LAG = 1
-OUT_LAG = 5
+OUT_LAG = 8
+RUN = 2
+assert X_LEAD % RUN == 0 and SAMPLE_TILES % RUN == 0 and OUT_LAG % RUN == 0
 
 FLOPS = 2 * PROJECTED * FEATURES * SAMPLES + 2 * 2 * NODES * CLASSES * PROJECTED * SAMPLES
 
@@ -40,14 +43,11 @@ def tile_bonsailayer_pa_t_kernel(tc, X, Z, W, V, th, out):
     nc = tc.nc
     with ExitStack() as ctx:
         keep = ctx.enter_context(tc.tile_pool(name="keep", bufs=1))
-        stage = ctx.enter_context(tc.tile_pool(name="stage", bufs=3))
-        codes_pool = ctx.enter_context(tc.tile_pool(name="codes", bufs=X_LEAD + 2))
+        stage = ctx.enter_context(tc.tile_pool(name="stage", bufs=6))
+        codes_pool = ctx.enter_context(tc.tile_pool(name="codes", bufs=4))
         work = ctx.enter_context(tc.tile_pool(name="work", bufs=3))
         product_pool = ctx.enter_context(tc.tile_pool(name="product", bufs=OUT_LAG + 2))
-        words_psum = ctx.enter_context(tc.psum_pool(name="words_psum", bufs=2))
-        xp_psum = ctx.enter_context(tc.psum_pool(name="xp_psum", bufs=1))
-        vx_psum = ctx.enter_context(tc.psum_pool(name="vx_psum", bufs=2))
-        wx_psum = ctx.enter_context(tc.psum_pool(name="wx_psum", bufs=2))
+        banks = ctx.enter_context(tc.psum_pool(name="banks", bufs=7))
         out_psum = ctx.enter_context(tc.psum_pool(name="out_psum", bufs=1))
         ctx.enter_context(tc.manual_schedule())
 
@@ -78,7 +78,7 @@ def tile_bonsailayer_pa_t_kernel(tc, X, Z, W, V, th, out):
 
         th_f32 = keep.tile([P, P], F32)
         nc.vector.tensor_copy(out=th_f32[:], in_=th_rows[:])
-        th_bank = words_psum.tile([P, P], F32, tag="words")
+        th_bank = banks.tile([P, P], F32, tag="bank")
         nc.tensor.transpose(th_bank[:], th_f32[:], identity[:])
         go_left = keep.tile([P, INTERNAL, SAMPLE_TILES], F32)
         go_right = keep.tile([P, INTERNAL, SAMPLE_TILES], F32)
@@ -100,41 +100,56 @@ def tile_bonsailayer_pa_t_kernel(tc, X, Z, W, V, th, out):
                 out=prob[:, 2 * n + 2, :], in0=prob[:, n, :], in1=go_right[:, n, :], op=ALU.mult
             )
 
-        def quantise_four_blocks(blocks, codes, scales):
-            bank = words_psum.tile([P, 2, 2, P], F32, tag="words")
+        def regroup(blocks, copy):
+            bank = banks.tile([P, 2, 2, P], F32, tag="bank")
             for slot in range(2):
                 for u in range(2):
                     nc.tensor.transpose(bank[:, slot, u, :], blocks[2 * slot + u], identity[:])
             grouped = stage.tile([P, 2 * P * PACK], BF16, tag="grouped", align_bytes=64)
-            nc.scalar.copy(
+            copy(
                 out=grouped[:].bitcast(F32).rearrange("p (s r u) -> p s r u", s=2, u=2),
                 in_=bank[:].rearrange("p s u r -> p s r u"),
             )
-            nc.vector.quantize_mx(out=codes.bitcast(FP8X4), scales=scales, in_=grouped[:])
+            return grouped
+
+        copiers = (nc.scalar.copy, nc.vector.tensor_copy)
+
+        def quantise_weights(jobs):
+            grouped = []
+            for k in range(len(jobs) + 1):
+                if k < len(jobs):
+                    grouped.append(regroup(jobs[k][0], copiers[k % 2]))
+                if k > 0:
+                    nc.vector.quantize_mx(
+                        out=jobs[k - 1][1].bitcast(FP8X4), scales=jobs[k - 1][2], in_=grouped[k - 1][:]
+                    )
 
         z_codes = keep.tile([P, PACK * X_PASSES * P], U32, align_bytes=64)
         z_scales = keep.tile([P, PACK * X_PASSES * P], U8, align_bytes=64)
+        z_jobs = []
         for t in range(PACK):
             z_words = z_rows[:, t, :].bitcast(F32)
             cols = slice(t * X_PASSES * P, (t + 1) * X_PASSES * P)
-            quantise_four_blocks(
-                [z_words[:, w * P : (w + 1) * P] for w in range(4)], z_codes[:, cols], z_scales[:, cols]
+            z_jobs.append(
+                ([z_words[:, w * P : (w + 1) * P] for w in range(4)], z_codes[:, cols], z_scales[:, cols])
             )
+        quantise_weights(z_jobs)
 
-        x_mx, xp_mx, products, out_banks = {}, {}, {}, {}
+        x_grouped, x_mx, xp_mx, products, out_banks = {}, {}, {}, {}, {}
+
+        def regroup_x(i):
+            x_words = x_rows[i // TILES_PER_LOAD][:, i % TILES_PER_LOAD, :].bitcast(F32)
+            x_grouped[i] = regroup([x_words[:, w * P : (w + 1) * P] for w in range(4)], copiers[i % 2])
 
         def quantise_x(i):
-            x_words = x_rows[i // TILES_PER_LOAD][:, i % TILES_PER_LOAD, :].bitcast(F32)
             x_codes = codes_pool.tile([P, X_PASSES * P], U32, tag="x_codes", align_bytes=64)
             x_scales = codes_pool.tile([P, X_PASSES * P], U8, tag="x_scales", align_bytes=64)
-            quantise_four_blocks(
-                [x_words[:, w * P : (w + 1) * P] for w in range(4)], x_codes[:], x_scales[:]
-            )
+            nc.vector.quantize_mx(out=x_codes[:].bitcast(FP8X4), scales=x_scales[:], in_=x_grouped[i][:])
             x_mx[i] = (x_codes, x_scales)
 
         def project(i):
             x_codes, x_scales = x_mx[i]
-            bank = xp_psum.tile([P, PACK, P], F32, tag="xp")
+            bank = banks.tile([P, PACK, P], F32, tag="bank")
             for t in range(PACK):
                 for c in range(X_PASSES):
                     z_cols = slice((t * X_PASSES + c) * P, (t * X_PASSES + c + 1) * P)
@@ -176,10 +191,10 @@ def tile_bonsailayer_pa_t_kernel(tc, X, Z, W, V, th, out):
                 done += width
 
         def score_nodes(i):
-            vx_low = vx_psum.tile([P, BANK], F32, tag="vx")
-            vx_high = vx_psum.tile([P, BANK], F32, tag="vx")
-            wx_low = wx_psum.tile([P, BANK], F32, tag="wx")
-            wx_high = wx_psum.tile([P, BANK], F32, tag="wx")
+            vx_low = banks.tile([P, BANK], F32, tag="bank")
+            vx_high = banks.tile([P, BANK], F32, tag="bank")
+            wx_low = banks.tile([P, BANK], F32, tag="bank")
+            wx_high = banks.tile([P, BANK], F32, tag="bank")
             multiply_nodes(vx_low, i, 0, LOW_WIDTHS)
             multiply_nodes(vx_high, i, LOW_NODES, HIGH_WIDTHS)
             multiply_nodes(wx_low, i, NODES, LOW_WIDTHS)
@@ -227,31 +242,42 @@ def tile_bonsailayer_pa_t_kernel(tc, X, Z, W, V, th, out):
         def is_tile(i):
             return 0 <= i < SAMPLE_TILES
 
-        def pipeline_step(step):
-            if is_tile(step + X_LEAD):
-                quantise_x(step + X_LEAD)
-            if is_tile(step - OUT_LAG):
-                transpose_score(step - OUT_LAG)
-            if is_tile(step + XP_LEAD):
-                project(step + XP_LEAD)
-            if is_tile(step):
-                score_nodes(step)
+        def fold_all(step):
             for f, (first, count) in enumerate(FOLDS):
                 if is_tile(step - FOLD_LAG - f):
                     fold_nodes(nc.gpsimd if f == 0 else nc.vector, step - FOLD_LAG - f, first, count)
 
-        for step in range(-X_LEAD, 0):
-            pipeline_step(step)
+        def pipeline_run(first):
+            steps = range(first, first + RUN)
+            for step in steps:
+                if is_tile(step + X_LEAD):
+                    regroup_x(step + X_LEAD)
+            for step in steps:
+                if is_tile(step - OUT_LAG):
+                    transpose_score(step - OUT_LAG)
+            for step in steps:
+                if is_tile(step + XQ_LEAD):
+                    quantise_x(step + XQ_LEAD)
+                if is_tile(step + XP_LEAD):
+                    project(step + XP_LEAD)
+                if is_tile(step):
+                    score_nodes(step)
+                fold_all(step)
+
+        for first in range(-X_LEAD, 0, RUN):
+            pipeline_run(first)
 
         vw_codes = keep.tile([P, 2 * NODES * P], U32, align_bytes=64)
         vw_scales = keep.tile([P, 2 * NODES * P], U8, align_bytes=64)
+        vw_jobs = []
         for pair in range(NODES):
             blocks = []
             for r in (2 * pair, 2 * pair + 1):
                 vw_words = vw_rows[:, r, :].bitcast(F32)
                 blocks.extend([vw_words[:, 0:P], vw_words[:, P : 2 * P]])
             cols = slice(2 * pair * P, (2 * pair + 2) * P)
-            quantise_four_blocks(blocks, vw_codes[:, cols], vw_scales[:, cols])
+            vw_jobs.append((blocks, vw_codes[:, cols], vw_scales[:, cols]))
+        quantise_weights(vw_jobs)
 
-        for step in range(0, SAMPLE_TILES + OUT_LAG):
-            pipeline_step(step)
+        for first in range(0, SAMPLE_TILES + OUT_LAG, RUN):
+            pipeline_run(first)

from contextlib import ExitStack

import concourse.mybir as mybir
from concourse.masks import make_identity

F32 = mybir.dt.float32
BF16 = mybir.dt.bfloat16
U32 = mybir.dt.uint32
U8 = mybir.dt.uint8
FP8X4 = mybir.dt.float8_e4m3fn_x4
ACT = mybir.ActivationFunctionType
ALU = mybir.AluOpType

P = 128
PACK = 4
K_PASS = P * PACK
BANK = 512

SAMPLES, FEATURES, PROJECTED, CLASSES = 4096, 1024, 512, 128
INTERNAL, NODES = 3, 7
SAMPLE_TILES = SAMPLES // P
TILES_PER_LOAD = 4
X_PASSES = FEATURES // K_PASS
LOW_NODES = BANK // CLASSES

LOW_WIDTHS = (512,)
HIGH_WIDTHS = (256, 128)

FOLDS = ((0, 3), (3, 2), (5, 1))

X_LEAD = 4
XQ_LEAD = 3
XP_LEAD = 2
FOLD_LAG = 1
OUT_LAG = 8
RUN = 2
assert X_LEAD % RUN == 0 and SAMPLE_TILES % RUN == 0 and OUT_LAG % RUN == 0

FLOPS = 2 * PROJECTED * FEATURES * SAMPLES + 2 * 2 * NODES * CLASSES * PROJECTED * SAMPLES


def tile_bonsailayer_pa_t_kernel(tc, X, Z, W, V, th, out):
    nc = tc.nc
    with ExitStack() as ctx:
        keep = ctx.enter_context(tc.tile_pool(name="keep", bufs=1))
        stage = ctx.enter_context(tc.tile_pool(name="stage", bufs=6))
        codes_pool = ctx.enter_context(tc.tile_pool(name="codes", bufs=4))
        work = ctx.enter_context(tc.tile_pool(name="work", bufs=3))
        product_pool = ctx.enter_context(tc.tile_pool(name="product", bufs=OUT_LAG + 2))
        banks = ctx.enter_context(tc.psum_pool(name="banks", bufs=7))
        out_psum = ctx.enter_context(tc.psum_pool(name="out_psum", bufs=1))
        ctx.enter_context(tc.manual_schedule())

        th_rows = keep.tile([P, P], BF16)
        nc.vector.memset(th_rows[:], 0.0)
        nc.sync.dma_start(
            out=th_rows[0 : INTERNAL * SAMPLE_TILES, :],
            in_=th.rearrange("n (i p) -> (n i) p", p=P),
        )
        z_rows = keep.tile([P, PACK, FEATURES], BF16)
        nc.sync.dma_start(
            out=z_rows[:].rearrange("p (u e) d -> p u e d", e=2),
            in_=Z.rearrange("(u p e) d -> p u e d", u=2, e=2),
        )
        x_loads = X.rearrange("(g j p) d -> g p j d", j=TILES_PER_LOAD, p=P)
        x_rows = []
        for g in range(SAMPLE_TILES // TILES_PER_LOAD):
            x_rows.append(keep.tile([P, TILES_PER_LOAD, FEATURES], BF16, name="x_rows%d" % g))
        nc.sync.dma_start(out=x_rows[0][:], in_=x_loads[0])
        vw_rows = keep.tile([P, 2 * NODES, PROJECTED], BF16)
        nc.sync.dma_start(out=vw_rows[:, 0:NODES, :], in_=V.rearrange("(n p) k -> p n k", p=P))
        nc.sync.dma_start(out=vw_rows[:, NODES:, :], in_=W.rearrange("(n p) k -> p n k", p=P))
        for g in range(1, SAMPLE_TILES // TILES_PER_LOAD):
            nc.sync.dma_start(out=x_rows[g][:], in_=x_loads[g])

        identity = keep.tile([P, P], F32)
        make_identity(nc, identity[:])

        th_f32 = keep.tile([P, P], F32)
        nc.vector.tensor_copy(out=th_f32[:], in_=th_rows[:])
        th_bank = banks.tile([P, P], F32, tag="bank")
        nc.tensor.transpose(th_bank[:], th_f32[:], identity[:])
        go_left = keep.tile([P, INTERNAL, SAMPLE_TILES], F32)
        go_right = keep.tile([P, INTERNAL, SAMPLE_TILES], F32)
        nc.vector.tensor_scalar(
            out=go_left[:].rearrange("p n i -> p (n i)"), in0=th_bank[:, 0 : INTERNAL * SAMPLE_TILES],
            scalar1=0.5, scalar2=0.5, op0=ALU.mult, op1=ALU.add,
        )
        nc.vector.tensor_scalar(
            out=go_right[:].rearrange("p n i -> p (n i)"), in0=th_bank[:, 0 : INTERNAL * SAMPLE_TILES],
            scalar1=-0.5, scalar2=0.5, op0=ALU.mult, op1=ALU.add,
        )
        prob = keep.tile([P, NODES, SAMPLE_TILES], F32)
        nc.vector.memset(prob[:, 0, :], 1.0)
        for n in range(INTERNAL):
            nc.vector.tensor_tensor(
                out=prob[:, 2 * n + 1, :], in0=prob[:, n, :], in1=go_left[:, n, :], op=ALU.mult
            )
            nc.vector.tensor_tensor(
                out=prob[:, 2 * n + 2, :], in0=prob[:, n, :], in1=go_right[:, n, :], op=ALU.mult
            )

        def regroup(blocks, copy):
            bank = banks.tile([P, 2, 2, P], F32, tag="bank")
            for slot in range(2):
                for u in range(2):
                    nc.tensor.transpose(bank[:, slot, u, :], blocks[2 * slot + u], identity[:])
            grouped = stage.tile([P, 2 * P * PACK], BF16, tag="grouped", align_bytes=64)
            copy(
                out=grouped[:].bitcast(F32).rearrange("p (s r u) -> p s r u", s=2, u=2),
                in_=bank[:].rearrange("p s u r -> p s r u"),
            )
            return grouped

        copiers = (nc.scalar.copy, nc.vector.tensor_copy)

        def quantise_weights(jobs):
            grouped = []
            for k in range(len(jobs) + 1):
                if k < len(jobs):
                    grouped.append(regroup(jobs[k][0], copiers[k % 2]))
                if k > 0:
                    nc.vector.quantize_mx(
                        out=jobs[k - 1][1].bitcast(FP8X4), scales=jobs[k - 1][2], in_=grouped[k - 1][:]
                    )

        z_codes = keep.tile([P, PACK * X_PASSES * P], U32, align_bytes=64)
        z_scales = keep.tile([P, PACK * X_PASSES * P], U8, align_bytes=64)
        z_jobs = []
        for t in range(PACK):
            z_words = z_rows[:, t, :].bitcast(F32)
            cols = slice(t * X_PASSES * P, (t + 1) * X_PASSES * P)
            z_jobs.append(
                ([z_words[:, w * P : (w + 1) * P] for w in range(4)], z_codes[:, cols], z_scales[:, cols])
            )
        quantise_weights(z_jobs)

        x_grouped, x_mx, xp_mx, products, out_banks = {}, {}, {}, {}, {}

        def regroup_x(i):
            x_words = x_rows[i // TILES_PER_LOAD][:, i % TILES_PER_LOAD, :].bitcast(F32)
            x_grouped[i] = regroup([x_words[:, w * P : (w + 1) * P] for w in range(4)], copiers[i % 2])

        def quantise_x(i):
            x_codes = codes_pool.tile([P, X_PASSES * P], U32, tag="x_codes", align_bytes=64)
            x_scales = codes_pool.tile([P, X_PASSES * P], U8, tag="x_scales", align_bytes=64)
            nc.vector.quantize_mx(out=x_codes[:].bitcast(FP8X4), scales=x_scales[:], in_=x_grouped[i][:])
            x_mx[i] = (x_codes, x_scales)

        def project(i):
            x_codes, x_scales = x_mx[i]
            bank = banks.tile([P, PACK, P], F32, tag="bank")
            for t in range(PACK):
                for c in range(X_PASSES):
                    z_cols = slice((t * X_PASSES + c) * P, (t * X_PASSES + c + 1) * P)
                    x_cols = slice(c * P, (c + 1) * P)
                    nc.tensor.matmul_mx(
                        out=bank[:, t, :],
                        lhsT=z_codes[:, z_cols].bitcast(FP8X4),
                        lhsT_scale=z_scales[:, z_cols],
                        rhs=x_codes[:, x_cols].bitcast(FP8X4),
                        rhs_scale=x_scales[:, x_cols],
                        start=(c == 0),
                        stop=(c == X_PASSES - 1),
                    )
            grouped = stage.tile([P, P, PACK], BF16, tag="xp_grouped", align_bytes=64)
            nc.scalar.activation(
                out=grouped[:], in_=bank[:].rearrange("p t b -> p b t"), func=ACT.Copy, scale=1.0 / PROJECTED
            )
            xp_codes = codes_pool.tile([P, P], U32, tag="xp_codes", align_bytes=64)
            xp_scales = codes_pool.tile([P, P], U8, tag="xp_scales", align_bytes=64)
            nc.vector.quantize_mx(
                out=xp_codes[:].bitcast(FP8X4), scales=xp_scales[:], in_=grouped[:].rearrange("p b t -> p (b t)")
            )
            xp_mx[i] = (xp_codes, xp_scales)

        def multiply_nodes(bank, i, first_row_tile, widths):
            xp_codes, xp_scales = xp_mx[i]
            done = 0
            for width in widths:
                vw_cols = slice(first_row_tile * P + done, first_row_tile * P + done + width)
                nc.tensor.matmul_mx(
                    out=bank[:, done : done + width],
                    lhsT=xp_codes[:].bitcast(FP8X4),
                    lhsT_scale=xp_scales[:],
                    rhs=vw_codes[:, vw_cols].bitcast(FP8X4),
                    rhs_scale=vw_scales[:, vw_cols],
                    start=True,
                    stop=True,
                )
                done += width

        def score_nodes(i):
            vx_low = banks.tile([P, BANK], F32, tag="bank")
            vx_high = banks.tile([P, BANK], F32, tag="bank")
            wx_low = banks.tile([P, BANK], F32, tag="bank")
            wx_high = banks.tile([P, BANK], F32, tag="bank")
            multiply_nodes(vx_low, i, 0, LOW_WIDTHS)
            multiply_nodes(vx_high, i, LOW_NODES, HIGH_WIDTHS)
            multiply_nodes(wx_low, i, NODES, LOW_WIDTHS)
            multiply_nodes(wx_high, i, NODES + LOW_NODES, HIGH_WIDTHS)
            tanh_vx = work.tile([P, NODES * CLASSES], F32, tag="tanh_vx")
            nc.scalar.activation(out=tanh_vx[:, 0:BANK], in_=vx_low[:], func=ACT.Tanh)
            nc.scalar.activation(
                out=tanh_vx[:, BANK:], in_=vx_high[:, 0 : NODES * CLASSES - BANK], func=ACT.Tanh
            )
            product = product_pool.tile([P, NODES * CLASSES], F32, tag="product")
            for n in range(NODES):
                wx = wx_low if n < LOW_NODES else wx_high
                bank_cols = slice((n % LOW_NODES) * CLASSES, (n % LOW_NODES + 1) * CLASSES)
                node_cols = slice(n * CLASSES, (n + 1) * CLASSES)
                nc.vector.scalar_tensor_tensor(
                    out=product[:, node_cols],
                    in0=wx[:, bank_cols],
                    scalar=prob[:, n, i : i + 1],
                    in1=tanh_vx[:, node_cols],
                    op0=ALU.mult,
                    op1=ALU.mult,
                )
            products[i] = product

        def fold_nodes(engine, i, first, count):
            low = slice(first * CLASSES, (first + count) * CLASSES)
            high = slice((first + count) * CLASSES, (first + 2 * count) * CLASSES)
            engine.tensor_tensor(
                out=products[i][:, high], in0=products[i][:, low], in1=products[i][:, high], op=ALU.add
            )

        def transpose_score(i):
            g, j = divmod(i, TILES_PER_LOAD)
            if j == 0:
                out_bank = out_psum.tile([P, TILES_PER_LOAD, P], F32, tag="out")
                out_banks[g] = out_bank
            nc.tensor.transpose(out_banks[g][:, j, :], products[i][:, (NODES - 1) * CLASSES :], identity[:])
            if j == TILES_PER_LOAD - 1:
                out_sb = work.tile([P, TILES_PER_LOAD * P], F32, tag="out_sb")
                nc.scalar.copy(out=out_sb[:], in_=out_banks[g][:].rearrange("p j b -> p (j b)"))
                nc.sync.dma_start(
                    out=out[:, g * TILES_PER_LOAD * P : (g + 1) * TILES_PER_LOAD * P], in_=out_sb[:]
                )

        def is_tile(i):
            return 0 <= i < SAMPLE_TILES

        def fold_all(step):
            for f, (first, count) in enumerate(FOLDS):
                if is_tile(step - FOLD_LAG - f):
                    fold_nodes(nc.gpsimd if f == 0 else nc.vector, step - FOLD_LAG - f, first, count)

        def pipeline_run(first):
            steps = range(first, first + RUN)
            for step in steps:
                if is_tile(step + X_LEAD):
                    regroup_x(step + X_LEAD)
            for step in steps:
                if is_tile(step - OUT_LAG):
                    transpose_score(step - OUT_LAG)
            for step in steps:
                if is_tile(step + XQ_LEAD):
                    quantise_x(step + XQ_LEAD)
                if is_tile(step + XP_LEAD):
                    project(step + XP_LEAD)
                if is_tile(step):
                    score_nodes(step)
                fold_all(step)

        for first in range(-X_LEAD, 0, RUN):
            pipeline_run(first)

        vw_codes = keep.tile([P, 2 * NODES * P], U32, align_bytes=64)
        vw_scales = keep.tile([P, 2 * NODES * P], U8, align_bytes=64)
        vw_jobs = []
        for pair in range(NODES):
            blocks = []
            for r in (2 * pair, 2 * pair + 1):
                vw_words = vw_rows[:, r, :].bitcast(F32)
                blocks.extend([vw_words[:, 0:P], vw_words[:, P : 2 * P]])
            cols = slice(2 * pair * P, (2 * pair + 2) * P)
            vw_jobs.append((blocks, vw_codes[:, cols], vw_scales[:, cols]))
        quantise_weights(vw_jobs)

        for first in range(0, SAMPLE_TILES + OUT_LAG, RUN):
            pipeline_run(first)
